import numpy as np
import ml_dtypes


def mxq(x, axis, fmt="e4m3"):
    dtype, down = {"e4m3": (ml_dtypes.float8_e4m3fn, 7), "e5m2": (ml_dtypes.float8_e5m2, 14)}[fmt]
    v = np.moveaxis(np.asarray(x, np.float32).astype(ml_dtypes.bfloat16).astype(np.float64), axis, -1)
    blocks = v.reshape(v.shape[:-1] + (-1, 32))
    amax = np.abs(blocks).max(-1, keepdims=True)
    byte = np.maximum(np.where(amax > 0, np.frexp(amax)[1] - 1 + 127, 0) - down, 1)
    scale = np.exp2(byte - 127.0)
    codes = (blocks / scale).astype(np.float32).astype(dtype).astype(np.float64)
    return np.moveaxis((codes * scale).reshape(v.shape), -1, axis)


WIDE = False


def mx_kscale(k):
    if not WIDE:
        return np.ones(k)
    levels = np.array([30, -30])
    if k % 512:
        return np.exp2(np.random.permutation(np.resize(levels, k // 32))).repeat(32)
    a = np.empty((k // 512, 16))
    for p in range(k // 512):
        a[p, :8] = np.random.permutation(np.resize(levels, 8))
        for g in range(8):
            far = levels[np.abs(levels - a[p, g]) >= 10]
            a[p, g + 8] = far[np.random.randint(len(far))]
    return np.exp2(a.ravel()).repeat(32)


BF16 = ml_dtypes.bfloat16


def bf(x):
    return np.asarray(x, np.float32).astype(BF16)


def f64(x):
    return np.asarray(x).astype(np.float64)


B, S, D, H, KV, HD = 1, 512, 2048, 16, 4, 128
HALF = HD // 2
ROPE_THETA = 500000.0


def make_freqs_cis():
    inv = 1.0 / ROPE_THETA ** (np.arange(0, HD, 2) / HD)
    ang = np.outer(np.arange(S), inv)
    return np.stack([np.cos(ang), np.sin(ang)], axis=-1)


def apply_rope(xh, fc):
    x2 = xh.reshape(xh.shape[:-1] + (HALF, 2))
    c, sn = fc[None, :, None, :, 0], fc[None, :, None, :, 1]
    real = x2[..., 0] * c - x2[..., 1] * sn
    imag = x2[..., 0] * sn + x2[..., 1] * c
    return np.concatenate([real, imag], axis=-1)


def setup_inputs():
    s = mx_kscale(D)
    w = 1.0 / np.sqrt(D)
    return {"x": bf(np.random.standard_normal((B, S, D)) * s),
            "wq": bf(np.random.standard_normal((H * HD, D)) * w / s),
            "wk": bf(np.random.standard_normal((KV * HD, D)) * w / s),
            "wv": bf(np.random.standard_normal((KV * HD, D)) * w / s),
            "freqs_cis": bf(make_freqs_cis())}


def reference(x, wq, wk, wv, freqs_cis):
    xm = mxq(f64(x), 2, "e5m2")
    fc = f64(freqs_cis)
    q = (xm @ mxq(f64(wq), 1, "e5m2").T).reshape(B, S, H, HD)
    k = (xm @ mxq(f64(wk), 1, "e5m2").T).reshape(B, S, KV, HD)
    v = (xm @ mxq(f64(wv), 1, "e5m2").T).reshape(B, S, KV, HD)
    return apply_rope(q, fc), apply_rope(k, fc), v

@@ -1,0 +1,240 @@
+from contextlib import ExitStack
+
+import concourse.mybir as mybir
+from concourse.masks import make_identity
+
+S, D, H, KV, HD = 512, 2048, 16, 4, 128
+FLOPS = 2 * S * D * (H + 2 * KV) * HD
+
+F32 = mybir.dt.float32
+BF16 = mybir.dt.bfloat16
+U32 = mybir.dt.uint32
+U8 = mybir.dt.uint8
+FP8X4 = mybir.dt.float8_e5m2_x4
+ALU = mybir.AluOpType
+
+P = 128
+PASSES = 4
+N = 512
+HALF_ROWS = 256
+WORDS = D // 2
+T_BANKS = 4
+M_BANKS = 4
+PERM = ["--","--","--","--","--","--","--","--","--","--","--","--","--","--"]
+G2, G4 = 0, 0
+EARLY = 0
+FULL = False
+
+
+def tile_attention_pa_kernel(tc, x, wq, wk, wv, freqs_cis, out_0, out_1, out_2):
+    nc = tc.nc
+    x2 = x.rearrange("b s d -> (b s) d")
+    q2 = out_0.rearrange("b s h d -> (b s) (h d)")
+    k2 = out_1.rearrange("b s h d -> (b s) (h d)")
+    v2 = out_2.rearrange("b s h d -> (b s) (h d)")
+    w_units = [wq[N * i : N * (i + 1), :] for i in range(4)] + [wk, wv]
+    o_units = [q2[:, N * i : N * (i + 1)] for i in range(4)] + [k2, v2]
+    V_UNIT = 5
+    X = "x"
+    halves = [(0, 0), (0, 1), (X, 0), (X, 1)] + [(u, a) for u in range(1, 6) for a in (0, 1)]
+    n_halves = len(halves)
+
+    with ExitStack() as ctx:
+        keep = ctx.enter_context(tc.tile_pool(name="keep", bufs=1))
+        raw_pool = ctx.enter_context(tc.tile_pool(name="raw", bufs=2 * n_halves))
+        perm_pool = ctx.enter_context(tc.tile_pool(name="perm", bufs=6))
+        grp_pool = ctx.enter_context(tc.tile_pool(name="grp", bufs=10))
+        code_pool = ctx.enter_context(tc.tile_pool(name="code", bufs=2))
+        prod_pool = ctx.enter_context(tc.tile_pool(name="prod", bufs=4))
+        out_pool = ctx.enter_context(tc.tile_pool(name="outp", bufs=12))
+        psum = ctx.enter_context(tc.psum_pool(name="psum", bufs=1))
+
+        ident = keep.tile([P, P], F32)
+        make_identity(nc, ident[:])
+
+        ctx.enter_context(tc.manual_schedule())
+
+        raw = {}
+        for h, (u, a) in enumerate(halves):
+            src = x2 if u == X else w_units[u]
+            for r in (0, 1):
+                t = raw_pool.tile([P, D], BF16, name="rawt", align_bytes=64)
+                row0 = HALF_ROWS * a + P * r
+                nc.sync.dma_start(out=t[:], in_=src[row0 : row0 + P, :])
+                raw[h, r] = t[:].bitcast(F32)
+
+        freq = keep.tile([P, 4, HD // 2, 2], BF16)
+        nc.scalar.dma_start(out=freq[:], in_=freqs_cis.rearrange("(m p) j e -> p m j e", p=P))
+        table = keep.tile([P, 4, 2, 2, HD // 2], F32)
+        nc.scalar.mul(table[:, :, 0, 1, :], freq[:, :, :, 1], -1.0)
+        nc.scalar.copy(table[:, :, 0, 0, :], freq[:, :, :, 0])
+        nc.scalar.copy(table[:, :, 1, 0, :], freq[:, :, :, 1])
+        nc.scalar.copy(table[:, :, 1, 1, :], freq[:, :, :, 0])
+
+        x_codes = keep.tile([P, PASSES, N], U32, align_bytes=64)
+        x_scales = keep.tile([P, PASSES, N], U8, align_bytes=64)
+        codes = {X: (x_codes, x_scales)}
+        sorted_words = {}
+        grouped = {}
+        count = {"t": 0, "m": 0, "perm": 0}
+        late = []
+        prods = {}
+        results = {}
+
+        def permute_to(last):
+            while count["perm"] <= min(last, n_halves - 1):
+                h = count["perm"]
+                count["perm"] += 1
+                for r in (0, 1):
+                    if PERM[h][r] == "-":
+                        continue
+                    t = perm_pool.tile([P, 2, WORDS // 2], F32, name="sorted")
+                    src = raw[h, r].rearrange("p (j u) -> p u j", u=2)
+                    if PERM[h][r] == "S":
+                        nc.scalar.copy(t[:], src)
+                    else:
+                        nc.vector.tensor_copy(out=t[:], in_=src)
+                    sorted_words[h, r] = t
+
+        def transpose(h):
+            for g in range(PASSES):
+                bank = psum.tile([P, 2, HALF_ROWS], F32, name="tb%d" % (count["t"] % T_BANKS))
+                count["t"] += 1
+                for r in (0, 1):
+                    for u in (0, 1):
+                        if (h, r) in sorted_words:
+                            src = sorted_words[h, r][:, u, P * g : P * (g + 1)]
+                        else:
+                            src = raw[h, r][:, 2 * P * g + u : 2 * P * (g + 1) : 2]
+                        nc.tensor.transpose(bank[:, u, P * r : P * (r + 1)], src, ident[:])
+                t = grp_pool.tile([P, HALF_ROWS, 2], F32, name="grouped", align_bytes=64)
+                nc.scalar.copy(t[:], bank[:].rearrange("p u n -> p n u"))
+                grouped[h, g] = t
+
+        def quantize(h, passes):
+            u, a = halves[h]
+            if u not in codes:
+                w_codes = code_pool.tile([P, PASSES, N], U32, align_bytes=64)
+                w_scales = code_pool.tile([P, PASSES, N], U8, align_bytes=64)
+                codes[u] = (w_codes, w_scales)
+            cols = slice(HALF_ROWS * a, HALF_ROWS * (a + 1))
+            for g in passes:
+                nc.vector.quantize_mx(
+                    out=codes[u][0][:, g, cols].bitcast(FP8X4),
+                    scales=codes[u][1][:, g, cols],
+                    in_=grouped[h, g][:].rearrange("p n u -> p (n u)").bitcast(BF16),
+                )
+
+        def store(u, m):
+            nc.sync.dma_start(out=o_units[u][P * m : P * (m + 1), :], in_=results[u, m][:])
+
+        def add_half(eng, u, m, w):
+            res = results[u, m][:].rearrange("p (h w j) -> p h w j", w=2, j=HD // 2)
+            prod = prods[u, m]
+            eng.tensor_tensor(out=res[:, :, w, :], in0=prod[:, w, :, 0, :], in1=prod[:, w, :, 1, :], op=ALU.add)
+
+        def add_whole(u, m):
+            res = results[u, m][:].rearrange("p (h w j) -> p h w j", w=2, j=HD // 2)
+            prod = prods[u, m][:].rearrange("p w h e j -> p h w e j")
+            nc.vector.tensor_tensor(out=res, in0=prod[:, :, :, 0, :], in1=prod[:, :, :, 1, :], op=ALU.add)
+
+        def flush():
+            while late:
+                u, m, w = late.pop(0)
+                if w == 0:
+                    late.pop(0)
+                    add_whole(u, m)
+                else:
+                    add_half(nc.vector, u, m, w)
+                store(u, m)
+
+        def project(u, tiles, n_gpsimd):
+            done = 0
+            for m in tiles:
+                acc = psum.tile([P, N], F32, name="mb%d" % (count["m"] % M_BANKS))
+                count["m"] += 1
+                for g in range(PASSES):
+                    nc.tensor.matmul_mx(
+                        out=acc[:],
+                        lhsT=x_codes[:, g, P * m : P * (m + 1)].bitcast(FP8X4),
+                        lhsT_scale=x_scales[:, g, P * m : P * (m + 1)],
+                        rhs=codes[u][0][:, g, :].bitcast(FP8X4),
+                        rhs_scale=codes[u][1][:, g, :],
+                        start=(g == 0),
+                        stop=(g == PASSES - 1),
+                    )
+                res = out_pool.tile([P, N], F32, name="res")
+                results[u, m] = res
+                if u == V_UNIT:
+                    if m % 2 == 0:
+                        nc.scalar.copy(res[:], acc[:])
+                    else:
+                        nc.vector.tensor_copy(out=res[:], in_=acc[:])
+                    store(u, m)
+                    continue
+                prod = prod_pool.tile([P, 2, 4, 2, HD // 2], F32, name="prod")
+                prods[u, m] = prod
+                y = acc[:].rearrange("p (h j e) -> p h e j", j=HD // 2, e=2)
+                for w in (0, 1):
+                    nc.vector.tensor_tensor(
+                        out=prod[:, w],
+                        in0=y,
+                        in1=table[:, m, w : w + 1].to_broadcast([P, 4, 2, HD // 2]),
+                        op=ALU.mult,
+                    )
+                    if done < n_gpsimd:
+                        add_half(nc.gpsimd, u, m, w)
+                        if w == 1:
+                            store(u, m)
+                    else:
+                        late.append((u, m, w))
+                    done += 1
+
+
+        all_passes = range(PASSES)
+        permute_to(0)
+        for h in range(4):
+            transpose(h)
+            permute_to(h + 1)
+            quantize(h, all_passes)
+        project(0, (0, 1), G2)
+        if FULL:
+            transpose(4)
+            permute_to(6)
+            flush()
+            quantize(4, all_passes)
+            project(0, (2, 3), G2)
+            for u in range(1, 6):
+                h = 2 * u + 3
+                transpose(h)
+                if h + 1 < n_halves:
+                    transpose(h + 1)
+                permute_to(h + 3)
+                for g in all_passes:
+                    if u > 1 and g >= EARLY:
+                        quantize(h - 1, [g])
+                    quantize(h, [g])
+                flush()
+                if h + 1 < n_halves:
+                    quantize(h + 1, range(EARLY))
+                project(u, (0, 1, 2, 3), G4)
+        else:
+            transpose(4)
+            permute_to(5)
+            flush()
+            quantize(4, all_passes)
+            project(0, (2, 3), G2)
+            transpose(5)
+            permute_to(6)
+            flush()
+            quantize(5, all_passes)
+            for u in range(1, 6):
+                for a in (0, 1):
+                    h = 2 * u + 4 + a
+                    if h < n_halves:
+                        transpose(h)
+                        permute_to(h + 1)
+                        quantize(h, all_passes)
+                    flush()
+                    project(u, (2 * a, 2 * a + 1), G2)
+        flush()

@@ -15,15 +15,18 @@ ALU = mybir.AluOpType
 
 P = 128
 PASSES = 4
+K_PASS = 512
 N = 512
-HALF_ROWS = 256
-WORDS = D // 2
 T_BANKS = 4
 M_BANKS = 4
-PERM = ["--","--","--","--","--","--","--","--","--","--","--","--","--","--"]
-G2, G4 = 0, 0
-EARLY = 0
-FULL = False
+HEAD = 12
+HEAD_SORT = "V"
+SORT = "S-"
+G_HALVES = 2
+G_SINGLE = 1
+AHEAD = 3
+WARM = 0
+WARM_MID = 0
 
 
 def tile_attention_pa_kernel(tc, x, wq, wk, wv, freqs_cis, out_0, out_1, out_2):
@@ -36,14 +39,18 @@ def tile_attention_pa_kernel(tc, x, wq, wk, wv, freqs_cis, out_0, out_1, out_2):
     o_units = [q2[:, N * i : N * (i + 1)] for i in range(4)] + [k2, v2]
     V_UNIT = 5
     X = "x"
-    halves = [(0, 0), (0, 1), (X, 0), (X, 1)] + [(u, a) for u in range(1, 6) for a in (0, 1)]
-    n_halves = len(halves)
+    chunks = []
+    for g in range(PASSES):
+        chunks += [(0, 0, 4, g), (X, 0, 2, g)]
+    chunks += [(X, 2 * P, 2, g) for g in range(PASSES)]
+    chunks += [(u, 0, 4, g) for u in range(1, 6) for g in range(PASSES)]
+    n_chunks = len(chunks)
 
     with ExitStack() as ctx:
         keep = ctx.enter_context(tc.tile_pool(name="keep", bufs=1))
-        raw_pool = ctx.enter_context(tc.tile_pool(name="raw", bufs=2 * n_halves))
-        perm_pool = ctx.enter_context(tc.tile_pool(name="perm", bufs=6))
-        grp_pool = ctx.enter_context(tc.tile_pool(name="grp", bufs=10))
+        raw_pool = ctx.enter_context(tc.tile_pool(name="raw", bufs=1))
+        sort_pool = ctx.enter_context(tc.tile_pool(name="sort", bufs=AHEAD + 2))
+        grp_pool = ctx.enter_context(tc.tile_pool(name="grp", bufs=5))
         code_pool = ctx.enter_context(tc.tile_pool(name="code", bufs=2))
         prod_pool = ctx.enter_context(tc.tile_pool(name="prod", bufs=4))
         out_pool = ctx.enter_context(tc.tile_pool(name="outp", bufs=12))
@@ -54,14 +61,13 @@ def tile_attention_pa_kernel(tc, x, wq, wk, wv, freqs_cis, out_0, out_1, out_2):
 
         ctx.enter_context(tc.manual_schedule())
 
-        raw = {}
-        for h, (u, a) in enumerate(halves):
+        raw = []
+        for i, (u, row0, tiles, g) in enumerate(chunks):
             src = x2 if u == X else w_units[u]
-            for r in (0, 1):
-                t = raw_pool.tile([P, D], BF16, name="rawt", align_bytes=64)
-                row0 = HALF_ROWS * a + P * r
-                nc.sync.dma_start(out=t[:], in_=src[row0 : row0 + P, :])
-                raw[h, r] = t[:].bitcast(F32)
+            t = raw_pool.tile([P, tiles, K_PASS], BF16, name="raw%d" % i, align_bytes=64)
+            rows = src[row0 : row0 + P * tiles, K_PASS * g : K_PASS * (g + 1)]
+            nc.sync.dma_start(out=t[:], in_=rows.rearrange("(r p) k -> p r k", p=P))
+            raw.append(t[:].rearrange("p r k -> p (r k)").bitcast(F32))
 
         freq = keep.tile([P, 4, HD // 2, 2], BF16)
         nc.scalar.dma_start(out=freq[:], in_=freqs_cis.rearrange("(m p) j e -> p m j e", p=P))
@@ -76,53 +82,57 @@ def tile_attention_pa_kernel(tc, x, wq, wk, wv, freqs_cis, out_0, out_1, out_2):
         codes = {X: (x_codes, x_scales)}
         sorted_words = {}
         grouped = {}
-        count = {"t": 0, "m": 0, "perm": 0}
+        count = {"t": 0, "m": 0, "sort": 0, "quant": 0}
         late = []
         prods = {}
         results = {}
+        accs = {}
 
-        def permute_to(last):
-            while count["perm"] <= min(last, n_halves - 1):
-                h = count["perm"]
-                count["perm"] += 1
-                for r in (0, 1):
-                    if PERM[h][r] == "-":
-                        continue
-                    t = perm_pool.tile([P, 2, WORDS // 2], F32, name="sorted")
-                    src = raw[h, r].rearrange("p (j u) -> p u j", u=2)
-                    if PERM[h][r] == "S":
-                        nc.scalar.copy(t[:], src)
-                    else:
-                        nc.vector.tensor_copy(out=t[:], in_=src)
-                    sorted_words[h, r] = t
+        def sort_to(last):
+            while count["sort"] <= min(last, n_chunks - 1):
+                i = count["sort"]
+                count["sort"] += 1
+                who = HEAD_SORT if i < HEAD else SORT[i % len(SORT)]
+                if who == "-":
+                    continue
+                t = sort_pool.tile([P, 2, P * chunks[i][2]], F32, name="sorted")
+                src = raw[i].rearrange("p (n u) -> p u n", u=2)
+                if who == "S":
+                    nc.scalar.copy(t[:], src)
+                else:
+                    nc.vector.tensor_copy(out=t[:], in_=src)
+                sorted_words[i] = t
 
-        def transpose(h):
-            for g in range(PASSES):
-                bank = psum.tile([P, 2, HALF_ROWS], F32, name="tb%d" % (count["t"] % T_BANKS))
+        def transpose(i):
+            tiles = chunks[i][2]
+            t = grp_pool.tile([P, P * tiles, 2], F32, name="grouped", align_bytes=64)
+            grouped[i] = t
+            for r0 in range(0, tiles, 2):
+                bank = psum.tile([P, 2, 2 * P], F32, name="tb%d" % (count["t"] % T_BANKS))
                 count["t"] += 1
-                for r in (0, 1):
+                for r in (r0, r0 + 1):
                     for u in (0, 1):
-                        if (h, r) in sorted_words:
-                            src = sorted_words[h, r][:, u, P * g : P * (g + 1)]
+                        if i in sorted_words:
+                            src = sorted_words[i][:, u, P * r : P * (r + 1)]
                         else:
-                            src = raw[h, r][:, 2 * P * g + u : 2 * P * (g + 1) : 2]
-                        nc.tensor.transpose(bank[:, u, P * r : P * (r + 1)], src, ident[:])
-                t = grp_pool.tile([P, HALF_ROWS, 2], F32, name="grouped", align_bytes=64)
-                nc.scalar.copy(t[:], bank[:].rearrange("p u n -> p n u"))
-                grouped[h, g] = t
+                            src = raw[i][:, 2 * P * r + u : 2 * P * (r + 1) : 2]
+                        nc.tensor.transpose(bank[:, u, P * (r - r0) : P * (r - r0 + 1)], src, ident[:])
+                nc.scalar.copy(t[:, P * r0 : P * (r0 + 2), :], bank[:].rearrange("p u n -> p n u"))
 
-        def quantize(h, passes):
-            u, a = halves[h]
-            if u not in codes:
-                w_codes = code_pool.tile([P, PASSES, N], U32, align_bytes=64)
-                w_scales = code_pool.tile([P, PASSES, N], U8, align_bytes=64)
-                codes[u] = (w_codes, w_scales)
-            cols = slice(HALF_ROWS * a, HALF_ROWS * (a + 1))
-            for g in passes:
+        def quantize_to(last):
+            while count["quant"] <= min(last, n_chunks - 1):
+                i = count["quant"]
+                count["quant"] += 1
+                u, row0, tiles, g = chunks[i]
+                if u not in codes:
+                    w_codes = code_pool.tile([P, PASSES, N], U32, align_bytes=64)
+                    w_scales = code_pool.tile([P, PASSES, N], U8, align_bytes=64)
+                    codes[u] = (w_codes, w_scales)
+                cols = slice(row0, row0 + P * tiles)
                 nc.vector.quantize_mx(
                     out=codes[u][0][:, g, cols].bitcast(FP8X4),
                     scales=codes[u][1][:, g, cols],
-                    in_=grouped[h, g][:].rearrange("p n u -> p (n u)").bitcast(BF16),
+                    in_=grouped[i][:].rearrange("p n u -> p (n u)").bitcast(BF16),
                 )
 
         def store(u, m):
@@ -148,93 +158,89 @@ def tile_attention_pa_kernel(tc, x, wq, wk, wv, freqs_cis, out_0, out_1, out_2):
                     add_half(nc.vector, u, m, w)
                 store(u, m)
 
-        def project(u, tiles, n_gpsimd):
-            done = 0
-            for m in tiles:
-                acc = psum.tile([P, N], F32, name="mb%d" % (count["m"] % M_BANKS))
+        def matmul_pass(u, m, g):
+            if g == 0:
+                accs[u, m] = psum.tile([P, N], F32, name="mb%d" % (count["m"] % M_BANKS))
                 count["m"] += 1
-                for g in range(PASSES):
-                    nc.tensor.matmul_mx(
-                        out=acc[:],
-                        lhsT=x_codes[:, g, P * m : P * (m + 1)].bitcast(FP8X4),
-                        lhsT_scale=x_scales[:, g, P * m : P * (m + 1)],
-                        rhs=codes[u][0][:, g, :].bitcast(FP8X4),
-                        rhs_scale=codes[u][1][:, g, :],
-                        start=(g == 0),
-                        stop=(g == PASSES - 1),
-                    )
-                res = out_pool.tile([P, N], F32, name="res")
-                results[u, m] = res
-                if u == V_UNIT:
-                    if m % 2 == 0:
-                        nc.scalar.copy(res[:], acc[:])
-                    else:
-                        nc.vector.tensor_copy(out=res[:], in_=acc[:])
-                    store(u, m)
-                    continue
-                prod = prod_pool.tile([P, 2, 4, 2, HD // 2], F32, name="prod")
-                prods[u, m] = prod
-                y = acc[:].rearrange("p (h j e) -> p h e j", j=HD // 2, e=2)
-                for w in (0, 1):
-                    nc.vector.tensor_tensor(
-                        out=prod[:, w],
-                        in0=y,
-                        in1=table[:, m, w : w + 1].to_broadcast([P, 4, 2, HD // 2]),
-                        op=ALU.mult,
-                    )
-                    if done < n_gpsimd:
-                        add_half(nc.gpsimd, u, m, w)
-                        if w == 1:
-                            store(u, m)
-                    else:
-                        late.append((u, m, w))
-                    done += 1
+            nc.tensor.matmul_mx(
+                out=accs[u, m][:],
+                lhsT=x_codes[:, g, P * m : P * (m + 1)].bitcast(FP8X4),
+                lhsT_scale=x_scales[:, g, P * m : P * (m + 1)],
+                rhs=codes[u][0][:, g, :].bitcast(FP8X4),
+                rhs_scale=codes[u][1][:, g, :],
+                start=(g == 0),
+                stop=(g == PASSES - 1),
+            )
 
+        def finish(u, m, n_gpsimd):
+            acc = accs[u, m]
+            res = out_pool.tile([P, N], F32, name="res")
+            results[u, m] = res
+            if u == V_UNIT:
+                if m % 2 == 0:
+                    nc.scalar.copy(res[:], acc[:])
+                else:
+                    nc.vector.tensor_copy(out=res[:], in_=acc[:])
+                store(u, m)
+                return
+            prod = prod_pool.tile([P, 2, 4, 2, HD // 2], F32, name="prod")
+            prods[u, m] = prod
+            y = acc[:].rearrange("p (h j e) -> p h e j", j=HD // 2, e=2)
+            for w in (0, 1):
+                nc.vector.tensor_tensor(
+                    out=prod[:, w],
+                    in0=y,
+                    in1=table[:, m, w : w + 1].to_broadcast([P, 4, 2, HD // 2]),
+                    op=ALU.mult,
+                )
+                if w < n_gpsimd:
+                    add_half(nc.gpsimd, u, m, w)
+                    if w == 1:
+                        store(u, m)
+                else:
+                    late.append((u, m, w))
 
-        all_passes = range(PASSES)
-        permute_to(0)
-        for h in range(4):
-            transpose(h)
-            permute_to(h + 1)
-            quantize(h, all_passes)
-        project(0, (0, 1), G2)
-        if FULL:
-            transpose(4)
-            permute_to(6)
-            flush()
-            quantize(4, all_passes)
-            project(0, (2, 3), G2)
-            for u in range(1, 6):
-                h = 2 * u + 3
-                transpose(h)
-                if h + 1 < n_halves:
-                    transpose(h + 1)
-                permute_to(h + 3)
-                for g in all_passes:
-                    if u > 1 and g >= EARLY:
-                        quantize(h - 1, [g])
-                    quantize(h, [g])
+        def group(u, m, n_gpsimd):
+            for g in range(PASSES):
+                matmul_pass(u, m, g)
+            finish(u, m, n_gpsimd)
+
+        def pair(u, a):
+            group(u, 2 * a, min(G_HALVES, 2))
+            group(u, 2 * a + 1, max(G_HALVES - 2, 0))
+
+        def head_pass(g):
+            matmul_pass(0, 0, g)
+            matmul_pass(0, 1, g)
+            if g == PASSES - 1:
+                finish(0, 0, min(G_HALVES, 2))
+                finish(0, 1, max(G_HALVES - 2, 0))
+
+        after = {}
+        for g in range(PASSES):
+            after[2 * g + 1 + 2] = (head_pass, (g,))
+        after[HEAD - 1 + 2] = (group, (0, 2, G_SINGLE))
+        after[HEAD + 1 + 2] = (group, (0, 3, G_SINGLE))
+        for u in range(1, V_UNIT):
+            last = HEAD + PASSES * u - 1
+            after[last + 2] = (pair, (u, 0))
+            after[last + 4] = (pair, (u, 1))
+        after[n_chunks] = (pair, (V_UNIT, 0))
+        after[n_chunks + 1] = (pair, (V_UNIT, 1))
+
+        sort_to(AHEAD - 1)
+        for i in range(n_chunks + 2):
+            if i < n_chunks:
+                transpose(i)
+                sort_to(i + AHEAD)
+            if i < HEAD:
                 flush()
-                if h + 1 < n_halves:
-                    quantize(h + 1, range(EARLY))
-                project(u, (0, 1, 2, 3), G4)
-        else:
-            transpose(4)
-            permute_to(5)
-            flush()
-            quantize(4, all_passes)
-            project(0, (2, 3), G2)
-            transpose(5)
-            permute_to(6)
-            flush()
-            quantize(5, all_passes)
-            for u in range(1, 6):
-                for a in (0, 1):
-                    h = 2 * u + 4 + a
-                    if h < n_halves:
-                        transpose(h)
-                        permute_to(h + 1)
-                        quantize(h, all_passes)
-                    flush()
-                    project(u, (2 * a, 2 * a + 1), G2)
+                quantize_to(i)
+            elif i in after:
+                quantize_to(count["quant"])
+                flush()
+                quantize_to(i)
+            if i in after:
+                fn, args = after[i]
+                fn(*args)
         flush()

from contextlib import ExitStack

import concourse.mybir as mybir
from concourse.masks import make_identity

S, D, H, KV, HD = 512, 2048, 16, 4, 128
FLOPS = 2 * S * D * (H + 2 * KV) * HD

F32 = mybir.dt.float32
BF16 = mybir.dt.bfloat16
U32 = mybir.dt.uint32
U8 = mybir.dt.uint8
FP8X4 = mybir.dt.float8_e5m2_x4
ALU = mybir.AluOpType

P = 128
PASSES = 4
K_PASS = 512
N = 512
T_BANKS = 4
M_BANKS = 4
HEAD = 12
HEAD_SORT = "V"
SORT = "S-"
G_HALVES = 2
G_SINGLE = 1
AHEAD = 3
WARM = 0
WARM_MID = 0


def tile_attention_pa_kernel(tc, x, wq, wk, wv, freqs_cis, out_0, out_1, out_2):
    nc = tc.nc
    x2 = x.rearrange("b s d -> (b s) d")
    q2 = out_0.rearrange("b s h d -> (b s) (h d)")
    k2 = out_1.rearrange("b s h d -> (b s) (h d)")
    v2 = out_2.rearrange("b s h d -> (b s) (h d)")
    w_units = [wq[N * i : N * (i + 1), :] for i in range(4)] + [wk, wv]
    o_units = [q2[:, N * i : N * (i + 1)] for i in range(4)] + [k2, v2]
    V_UNIT = 5
    X = "x"
    chunks = []
    for g in range(PASSES):
        chunks += [(0, 0, 4, g), (X, 0, 2, g)]
    chunks += [(X, 2 * P, 2, g) for g in range(PASSES)]
    chunks += [(u, 0, 4, g) for u in range(1, 6) for g in range(PASSES)]
    n_chunks = len(chunks)

    with ExitStack() as ctx:
        keep = ctx.enter_context(tc.tile_pool(name="keep", bufs=1))
        raw_pool = ctx.enter_context(tc.tile_pool(name="raw", bufs=1))
        sort_pool = ctx.enter_context(tc.tile_pool(name="sort", bufs=AHEAD + 2))
        grp_pool = ctx.enter_context(tc.tile_pool(name="grp", bufs=5))
        code_pool = ctx.enter_context(tc.tile_pool(name="code", bufs=2))
        prod_pool = ctx.enter_context(tc.tile_pool(name="prod", bufs=4))
        out_pool = ctx.enter_context(tc.tile_pool(name="outp", bufs=12))
        psum = ctx.enter_context(tc.psum_pool(name="psum", bufs=1))

        ident = keep.tile([P, P], F32)
        make_identity(nc, ident[:])

        ctx.enter_context(tc.manual_schedule())

        raw = []
        for i, (u, row0, tiles, g) in enumerate(chunks):
            src = x2 if u == X else w_units[u]
            t = raw_pool.tile([P, tiles, K_PASS], BF16, name="raw%d" % i, align_bytes=64)
            rows = src[row0 : row0 + P * tiles, K_PASS * g : K_PASS * (g + 1)]
            nc.sync.dma_start(out=t[:], in_=rows.rearrange("(r p) k -> p r k", p=P))
            raw.append(t[:].rearrange("p r k -> p (r k)").bitcast(F32))

        freq = keep.tile([P, 4, HD // 2, 2], BF16)
        nc.scalar.dma_start(out=freq[:], in_=freqs_cis.rearrange("(m p) j e -> p m j e", p=P))
        table = keep.tile([P, 4, 2, 2, HD // 2], F32)
        nc.scalar.mul(table[:, :, 0, 1, :], freq[:, :, :, 1], -1.0)
        nc.scalar.copy(table[:, :, 0, 0, :], freq[:, :, :, 0])
        nc.scalar.copy(table[:, :, 1, 0, :], freq[:, :, :, 1])
        nc.scalar.copy(table[:, :, 1, 1, :], freq[:, :, :, 0])

        x_codes = keep.tile([P, PASSES, N], U32, align_bytes=64)
        x_scales = keep.tile([P, PASSES, N], U8, align_bytes=64)
        codes = {X: (x_codes, x_scales)}
        sorted_words = {}
        grouped = {}
        count = {"t": 0, "m": 0, "sort": 0, "quant": 0}
        late = []
        prods = {}
        results = {}
        accs = {}

        def sort_to(last):
            while count["sort"] <= min(last, n_chunks - 1):
                i = count["sort"]
                count["sort"] += 1
                who = HEAD_SORT if i < HEAD else SORT[i % len(SORT)]
                if who == "-":
                    continue
                t = sort_pool.tile([P, 2, P * chunks[i][2]], F32, name="sorted")
                src = raw[i].rearrange("p (n u) -> p u n", u=2)
                if who == "S":
                    nc.scalar.copy(t[:], src)
                else:
                    nc.vector.tensor_copy(out=t[:], in_=src)
                sorted_words[i] = t

        def transpose(i):
            tiles = chunks[i][2]
            t = grp_pool.tile([P, P * tiles, 2], F32, name="grouped", align_bytes=64)
            grouped[i] = t
            for r0 in range(0, tiles, 2):
                bank = psum.tile([P, 2, 2 * P], F32, name="tb%d" % (count["t"] % T_BANKS))
                count["t"] += 1
                for r in (r0, r0 + 1):
                    for u in (0, 1):
                        if i in sorted_words:
                            src = sorted_words[i][:, u, P * r : P * (r + 1)]
                        else:
                            src = raw[i][:, 2 * P * r + u : 2 * P * (r + 1) : 2]
                        nc.tensor.transpose(bank[:, u, P * (r - r0) : P * (r - r0 + 1)], src, ident[:])
                nc.scalar.copy(t[:, P * r0 : P * (r0 + 2), :], bank[:].rearrange("p u n -> p n u"))

        def quantize_to(last):
            while count["quant"] <= min(last, n_chunks - 1):
                i = count["quant"]
                count["quant"] += 1
                u, row0, tiles, g = chunks[i]
                if u not in codes:
                    w_codes = code_pool.tile([P, PASSES, N], U32, align_bytes=64)
                    w_scales = code_pool.tile([P, PASSES, N], U8, align_bytes=64)
                    codes[u] = (w_codes, w_scales)
                cols = slice(row0, row0 + P * tiles)
                nc.vector.quantize_mx(
                    out=codes[u][0][:, g, cols].bitcast(FP8X4),
                    scales=codes[u][1][:, g, cols],
                    in_=grouped[i][:].rearrange("p n u -> p (n u)").bitcast(BF16),
                )

        def store(u, m):
            nc.sync.dma_start(out=o_units[u][P * m : P * (m + 1), :], in_=results[u, m][:])

        def add_half(eng, u, m, w):
            res = results[u, m][:].rearrange("p (h w j) -> p h w j", w=2, j=HD // 2)
            prod = prods[u, m]
            eng.tensor_tensor(out=res[:, :, w, :], in0=prod[:, w, :, 0, :], in1=prod[:, w, :, 1, :], op=ALU.add)

        def add_whole(u, m):
            res = results[u, m][:].rearrange("p (h w j) -> p h w j", w=2, j=HD // 2)
            prod = prods[u, m][:].rearrange("p w h e j -> p h w e j")
            nc.vector.tensor_tensor(out=res, in0=prod[:, :, :, 0, :], in1=prod[:, :, :, 1, :], op=ALU.add)

        def flush():
            while late:
                u, m, w = late.pop(0)
                if w == 0:
                    late.pop(0)
                    add_whole(u, m)
                else:
                    add_half(nc.vector, u, m, w)
                store(u, m)

        def matmul_pass(u, m, g):
            if g == 0:
                accs[u, m] = psum.tile([P, N], F32, name="mb%d" % (count["m"] % M_BANKS))
                count["m"] += 1
            nc.tensor.matmul_mx(
                out=accs[u, m][:],
                lhsT=x_codes[:, g, P * m : P * (m + 1)].bitcast(FP8X4),
                lhsT_scale=x_scales[:, g, P * m : P * (m + 1)],
                rhs=codes[u][0][:, g, :].bitcast(FP8X4),
                rhs_scale=codes[u][1][:, g, :],
                start=(g == 0),
                stop=(g == PASSES - 1),
            )

        def finish(u, m, n_gpsimd):
            acc = accs[u, m]
            res = out_pool.tile([P, N], F32, name="res")
            results[u, m] = res
            if u == V_UNIT:
                if m % 2 == 0:
                    nc.scalar.copy(res[:], acc[:])
                else:
                    nc.vector.tensor_copy(out=res[:], in_=acc[:])
                store(u, m)
                return
            prod = prod_pool.tile([P, 2, 4, 2, HD // 2], F32, name="prod")
            prods[u, m] = prod
            y = acc[:].rearrange("p (h j e) -> p h e j", j=HD // 2, e=2)
            for w in (0, 1):
                nc.vector.tensor_tensor(
                    out=prod[:, w],
                    in0=y,
                    in1=table[:, m, w : w + 1].to_broadcast([P, 4, 2, HD // 2]),
                    op=ALU.mult,
                )
                if w < n_gpsimd:
                    add_half(nc.gpsimd, u, m, w)
                    if w == 1:
                        store(u, m)
                else:
                    late.append((u, m, w))

        def group(u, m, n_gpsimd):
            for g in range(PASSES):
                matmul_pass(u, m, g)
            finish(u, m, n_gpsimd)

        def pair(u, a):
            group(u, 2 * a, min(G_HALVES, 2))
            group(u, 2 * a + 1, max(G_HALVES - 2, 0))

        def head_pass(g):
            matmul_pass(0, 0, g)
            matmul_pass(0, 1, g)
            if g == PASSES - 1:
                finish(0, 0, min(G_HALVES, 2))
                finish(0, 1, max(G_HALVES - 2, 0))

        after = {}
        for g in range(PASSES):
            after[2 * g + 1 + 2] = (head_pass, (g,))
        after[HEAD - 1 + 2] = (group, (0, 2, G_SINGLE))
        after[HEAD + 1 + 2] = (group, (0, 3, G_SINGLE))
        for u in range(1, V_UNIT):
            last = HEAD + PASSES * u - 1
            after[last + 2] = (pair, (u, 0))
            after[last + 4] = (pair, (u, 1))
        after[n_chunks] = (pair, (V_UNIT, 0))
        after[n_chunks + 1] = (pair, (V_UNIT, 1))

        sort_to(AHEAD - 1)
        for i in range(n_chunks + 2):
            if i < n_chunks:
                transpose(i)
                sort_to(i + AHEAD)
            if i < HEAD:
                flush()
                quantize_to(i)
            elif i in after:
                quantize_to(count["quant"])
                flush()
                quantize_to(i)
            if i in after:
                fn, args = after[i]
                fn(*args)
        flush()
